import numpy as np
import ml_dtypes

BF16 = ml_dtypes.bfloat16


def bf(x):
    return np.asarray(x, np.float32).astype(BF16)


def f32(x):
    return np.asarray(x, np.float32)


def f64(x):
    return np.asarray(x).astype(np.float64)


def striped(idx):
    return np.tile(idx.reshape(-1, 16).T, (8, 1))


H, D, C, S, N, W = 2, 128, 256, 256, 128, 32


def setup_inputs():
    return {"base": f32(np.random.standard_normal((C, S))), "q": bf(np.random.standard_normal((C, N))), "k": bf(np.random.standard_normal((C, N))), "v": bf(np.random.standard_normal((N, C))), "offs": striped(np.random.permutation(S)[:N])}


def reference(base, q, k, v, offs):
    idx = offs[:16].T.reshape(-1)
    qh = f64(q).reshape(H, D, N)
    kh = f64(k).reshape(H, D, N)
    vh = f64(v).reshape(N, H, D)
    s = np.einsum("hdt,hdn->htn", kh, qh) / np.sqrt(D)
    key = np.arange(N)[:, None]
    qry = np.arange(N)[None, :]
    allowed = (key <= qry) & (key > qry - W)
    e = np.where(allowed[None, :, :], np.exp(s), 0.0)
    den = e.sum(axis=1)
    ctx = np.einsum("thd,htn->hdn", vh, e)
    res = ctx * (1.0 / den)[:, None, :]
    out = f64(base).copy()
    out[:, idx] = res.reshape(C, N)
    return out

@@ -1,0 +1,73 @@
+import math
+
+import concourse.mybir as mybir
+from concourse.masks import make_identity
+
+H, D, N, S, W = 2, 128, 128, 256, 32
+BF16, F32, U16 = mybir.dt.bfloat16, mybir.dt.float32, mybir.dt.uint16
+EXP = mybir.ActivationFunctionType.Exp
+MULT = mybir.AluOpType.mult
+IS_GE = mybir.AluOpType.is_ge
+
+MASKED = -30000.0
+
+FLOPS = 4 * H * D * sum(min(j + 1, W) for j in range(N))
+
+
+def tile_multiheadattn_kernel(tc, base, q, k, v, offs, out):
+    nc = tc.nc
+    with (
+        tc.tile_pool(name="held", bufs=1) as held,
+        tc.tile_pool(name="work", bufs=H) as work,
+        tc.psum_pool(name="psum", bufs=H) as psum,
+    ):
+        queues = [nc.sync, nc.scalar]
+        k_sb = [held.tile([D, N], BF16, name=f"k{h}") for h in range(H)]
+        q_sb = [held.tile([D, N], BF16, name=f"q{h}") for h in range(H)]
+        windows = [held.tile([D, S], F32, name=f"window{h}") for h in range(H)]
+        for h in range(H):
+            queues[h].dma_start(k_sb[h][:], k[h * D : (h + 1) * D, :])
+            queues[h].dma_start(q_sb[h][:], q[h * D : (h + 1) * D, :])
+        v_sb = held.tile([N, H * D], BF16, name="v_sb")
+        nc.sync.dma_start(v_sb[:], v)
+        offsets = held.tile([128, N // 16], U16, name="offsets")
+        nc.sync.dma_start(offsets[:], offs)
+        for h in range(H):
+            queues[h].dma_start(windows[h][:], base[h * D : (h + 1) * D, :])
+
+        mask_f32 = held.tile([N, N], F32, name="mask_f32")
+        nc.vector.memset(mask_f32[:], 0.0)
+        nc.gpsimd.affine_select(
+            out=mask_f32[:], in_=mask_f32[:], pattern=[[1, N]], compare_op=IS_GE, fill=MASKED, base=0, channel_multiplier=-1
+        )
+        nc.gpsimd.affine_select(
+            out=mask_f32[:], in_=mask_f32[:], pattern=[[-1, N]], compare_op=IS_GE, fill=MASKED, base=W - 1, channel_multiplier=1
+        )
+        mask = held.tile([N, N], BF16, name="mask")
+        nc.vector.tensor_copy(mask[:], mask_f32[:])
+        identity = held.tile([N, N], BF16, name="identity")
+        nc.vector.memset(identity[:], 0.0)
+        make_identity(nc, identity[:], nomemset=True)
+        ones = held.tile([N, D], BF16, name="ones")
+        nc.vector.memset(ones[:], 1.0)
+
+        for h in range(H):
+            scores = psum.tile([N, N], F32, name="scores")
+            nc.tensor.matmul(scores[:], identity[:], mask[:], start=True, stop=False)
+            nc.tensor.matmul(scores[:], k_sb[h][:], q_sb[h][:], start=False, stop=True)
+
+            e = work.tile([N, N], BF16, name="e")
+            nc.scalar.activation(e[:], scores[:], EXP, scale=1.0 / math.sqrt(D))
+
+            ctx_ps = psum.tile([D, N], F32, name="ctx_ps")
+            nc.tensor.matmul(ctx_ps[:], v_sb[:, h * D : (h + 1) * D], e[:], start=True, stop=True)
+            den_ps = psum.tile([D, N], F32, name="den_ps")
+            nc.tensor.matmul(den_ps[:], ones[:], e[:], start=True, stop=True)
+
+            ctx_sb = work.tile([D, N], F32, name="ctx_sb")
+            nc.scalar.copy(ctx_sb[:], ctx_ps[:])
+            inv_den = work.tile([D, N], F32, name="inv_den")
+            nc.vector.reciprocal(inv_den[:], den_ps[:])
+
+            nc.vector.tensor_tensor(windows[h][:].indirect(offsets[:]), ctx_sb[:], inv_den[:], MULT)
+            queues[h].dma_start(out[h * D : (h + 1) * D, :], windows[h][:])

@@ -4,6 +4,9 @@ import concourse.mybir as mybir
 from concourse.masks import make_identity
 
 H, D, N, S, W = 2, 128, 128, 256, 32
+P = 128
+G = H * D // P
+ROWS = P // H
 BF16, F32, U16 = mybir.dt.bfloat16, mybir.dt.float32, mybir.dt.uint16
 EXP = mybir.ActivationFunctionType.Exp
 MULT = mybir.AluOpType.mult
@@ -16,27 +19,27 @@ FLOPS = 4 * H * D * sum(min(j + 1, W) for j in range(N))
 
 def tile_multiheadattn_kernel(tc, base, q, k, v, offs, out):
     nc = tc.nc
+    base_tiles = base.rearrange("(p g) s -> g p s", g=G)
+    out_tiles = out.rearrange("(p g) s -> g p s", g=G)
     with (
         tc.tile_pool(name="held", bufs=1) as held,
-        tc.tile_pool(name="work", bufs=H) as work,
-        tc.psum_pool(name="psum", bufs=H) as psum,
+        tc.psum_pool(name="psum", bufs=1) as psum,
     ):
         queues = [nc.sync, nc.scalar]
-        k_sb = [held.tile([D, N], BF16, name=f"k{h}") for h in range(H)]
-        q_sb = [held.tile([D, N], BF16, name=f"q{h}") for h in range(H)]
-        windows = [held.tile([D, S], F32, name=f"window{h}") for h in range(H)]
-        for h in range(H):
-            queues[h].dma_start(k_sb[h][:], k[h * D : (h + 1) * D, :])
-            queues[h].dma_start(q_sb[h][:], q[h * D : (h + 1) * D, :])
+        k_sb = held.tile([D, H, N], BF16, name="k_sb")
+        nc.sync.dma_start(k_sb[:], k.rearrange("(h d) t -> d h t", h=H))
+        q_sb = held.tile([D, H, N], BF16, name="q_sb")
+        nc.scalar.dma_start(q_sb[:], q.rearrange("(h d) t -> d h t", h=H))
         v_sb = held.tile([N, H * D], BF16, name="v_sb")
         nc.sync.dma_start(v_sb[:], v)
-        offsets = held.tile([128, N // 16], U16, name="offsets")
+        offsets = held.tile([P, N // 16], U16, name="offsets")
         nc.sync.dma_start(offsets[:], offs)
-        for h in range(H):
-            queues[h].dma_start(windows[h][:], base[h * D : (h + 1) * D, :])
+        windows = [held.tile([P, S], F32, name=f"window{g}") for g in range(G)]
+        for g in range(G):
+            queues[g].dma_start(windows[g][:], base_tiles[g])
 
         mask_f32 = held.tile([N, N], F32, name="mask_f32")
-        nc.vector.memset(mask_f32[:], 0.0)
+        nc.gpsimd.memset(mask_f32[:], 0.0)
         nc.gpsimd.affine_select(
             out=mask_f32[:], in_=mask_f32[:], pattern=[[1, N]], compare_op=IS_GE, fill=MASKED, base=0, channel_multiplier=-1
         )
@@ -48,26 +51,32 @@ def tile_multiheadattn_kernel(tc, base, q, k, v, offs, out):
         identity = held.tile([N, N], BF16, name="identity")
         nc.vector.memset(identity[:], 0.0)
         make_identity(nc, identity[:], nomemset=True)
-        ones = held.tile([N, D], BF16, name="ones")
+        ones = held.tile([N, ROWS], BF16, name="ones")
         nc.vector.memset(ones[:], 1.0)
 
+        scores = psum.tile([N, H, N], F32, name="scores")
+        nc.tensor.matmul(scores[:], identity[:], mask[:].unsqueeze(1).to_broadcast([N, H, N]), start=True, stop=False)
         for h in range(H):
-            scores = psum.tile([N, N], F32, name="scores")
-            nc.tensor.matmul(scores[:], identity[:], mask[:], start=True, stop=False)
-            nc.tensor.matmul(scores[:], k_sb[h][:], q_sb[h][:], start=False, stop=True)
+            nc.tensor.matmul(scores[:, h, :], k_sb[:, h, :], q_sb[:, h, :], start=False, stop=(h == H - 1))
 
-            e = work.tile([N, N], BF16, name="e")
-            nc.scalar.activation(e[:], scores[:], EXP, scale=1.0 / math.sqrt(D))
+        e = held.tile([N, H, N], BF16, name="e")
+        nc.scalar.activation(e[:], scores[:], EXP, scale=1.0 / math.sqrt(D))
 
-            ctx_ps = psum.tile([D, N], F32, name="ctx_ps")
-            nc.tensor.matmul(ctx_ps[:], v_sb[:, h * D : (h + 1) * D], e[:], start=True, stop=True)
-            den_ps = psum.tile([D, N], F32, name="den_ps")
-            nc.tensor.matmul(den_ps[:], ones[:], e[:], start=True, stop=True)
+        den = psum.tile([P, N], F32, name="den")
+        for h in range(H):
+            nc.tensor.matmul(den[h * ROWS : (h + 1) * ROWS, :], ones[:], e[:, h, :], start=True, stop=True)
+        inv_den = held.tile([P, N], F32, name="inv_den")
+        nc.vector.reciprocal(inv_den[:], den[:])
 
-            ctx_sb = work.tile([D, N], F32, name="ctx_sb")
-            nc.scalar.copy(ctx_sb[:], ctx_ps[:])
-            inv_den = work.tile([D, N], F32, name="inv_den")
-            nc.vector.reciprocal(inv_den[:], den_ps[:])
+        v_tiles = v_sb[:].rearrange("t (p g) -> t g p", g=G)
+        ctx_sb = [held.tile([P, N], F32, name=f"ctx_sb{g}") for g in range(G)]
+        for g in range(G):
+            ctx_ps = psum.tile([P, N], F32, name=f"ctx_ps{g}")
+            for h in range(H):
+                rows = slice(h * ROWS, (h + 1) * ROWS)
+                nc.tensor.matmul(ctx_ps[rows, :], v_tiles[:, g, rows], e[:, h, :], start=True, stop=True)
+            nc.scalar.copy(ctx_sb[g][:], ctx_ps[:])
 
-            nc.vector.tensor_tensor(windows[h][:].indirect(offsets[:]), ctx_sb[:], inv_den[:], MULT)
-            queues[h].dma_start(out[h * D : (h + 1) * D, :], windows[h][:])
+        for g in range(G):
+            nc.vector.tensor_tensor(windows[g][:].indirect(offsets[:]), ctx_sb[g][:], inv_den[:], MULT)
+            queues[g].dma_start(out_tiles[g], windows[g][:])

@@ -4,9 +4,6 @@ import concourse.mybir as mybir
 from concourse.masks import make_identity
 
 H, D, N, S, W = 2, 128, 128, 256, 32
-P = 128
-G = H * D // P
-ROWS = P // H
 BF16, F32, U16 = mybir.dt.bfloat16, mybir.dt.float32, mybir.dt.uint16
 EXP = mybir.ActivationFunctionType.Exp
 MULT = mybir.AluOpType.mult
@@ -19,24 +16,24 @@ FLOPS = 4 * H * D * sum(min(j + 1, W) for j in range(N))
 
 def tile_multiheadattn_kernel(tc, base, q, k, v, offs, out):
     nc = tc.nc
-    base_tiles = base.rearrange("(p g) s -> g p s", g=G)
-    out_tiles = out.rearrange("(p g) s -> g p s", g=G)
     with (
         tc.tile_pool(name="held", bufs=1) as held,
-        tc.psum_pool(name="psum", bufs=1) as psum,
+        tc.tile_pool(name="work", bufs=H) as work,
+        tc.psum_pool(name="psum", bufs=H) as psum,
     ):
         queues = [nc.sync, nc.scalar]
-        k_sb = held.tile([D, H, N], BF16, name="k_sb")
-        nc.sync.dma_start(k_sb[:], k.rearrange("(h d) t -> d h t", h=H))
-        q_sb = held.tile([D, H, N], BF16, name="q_sb")
-        nc.scalar.dma_start(q_sb[:], q.rearrange("(h d) t -> d h t", h=H))
+        k_sb = [held.tile([D, N], BF16, name=f"k{h}") for h in range(H)]
+        q_sb = [held.tile([D, N], BF16, name=f"q{h}") for h in range(H)]
+        windows = [held.tile([D, S], F32, name=f"window{h}") for h in range(H)]
+        for h in range(H):
+            queues[h].dma_start(k_sb[h][:], k[h * D : (h + 1) * D, :])
+            queues[h].dma_start(q_sb[h][:], q[h * D : (h + 1) * D, :])
         v_sb = held.tile([N, H * D], BF16, name="v_sb")
         nc.sync.dma_start(v_sb[:], v)
-        offsets = held.tile([P, N // 16], U16, name="offsets")
+        offsets = held.tile([128, N // 16], U16, name="offsets")
         nc.sync.dma_start(offsets[:], offs)
-        windows = [held.tile([P, S], F32, name=f"window{g}") for g in range(G)]
-        for g in range(G):
-            queues[g].dma_start(windows[g][:], base_tiles[g])
+        for h in range(H):
+            queues[h].dma_start(windows[h][:], base[h * D : (h + 1) * D, :])
 
         mask_f32 = held.tile([N, N], F32, name="mask_f32")
         nc.gpsimd.memset(mask_f32[:], 0.0)
@@ -48,35 +45,36 @@ def tile_multiheadattn_kernel(tc, base, q, k, v, offs, out):
         )
         mask = held.tile([N, N], BF16, name="mask")
         nc.vector.tensor_copy(mask[:], mask_f32[:])
+        identity_f32 = held.tile([N, N], F32, name="identity_f32")
+        nc.vector.memset(identity_f32[:], 0.0)
+        make_identity(nc, identity_f32[:], nomemset=True)
         identity = held.tile([N, N], BF16, name="identity")
-        nc.vector.memset(identity[:], 0.0)
-        make_identity(nc, identity[:], nomemset=True)
-        ones = held.tile([N, ROWS], BF16, name="ones")
+        nc.vector.tensor_copy(identity[:], identity_f32[:])
+        ones = held.tile([N, 1], BF16, name="ones")
         nc.vector.memset(ones[:], 1.0)
 
-        scores = psum.tile([N, H, N], F32, name="scores")
-        nc.tensor.matmul(scores[:], identity[:], mask[:].unsqueeze(1).to_broadcast([N, H, N]), start=True, stop=False)
         for h in range(H):
-            nc.tensor.matmul(scores[:, h, :], k_sb[:, h, :], q_sb[:, h, :], start=False, stop=(h == H - 1))
+            scores = psum.tile([N, N], F32, name="scores")
+            nc.tensor.matmul(scores[:], identity[:], mask[:], start=True, stop=False)
+            nc.tensor.matmul(scores[:], k_sb[h][:], q_sb[h][:], start=False, stop=True)
 
-        e = held.tile([N, H, N], BF16, name="e")
-        nc.scalar.activation(e[:], scores[:], EXP, scale=1.0 / math.sqrt(D))
+            e = work.tile([N, N], BF16, name="e")
+            nc.scalar.activation(e[:], scores[:], EXP, scale=1.0 / math.sqrt(D))
 
-        den = psum.tile([P, N], F32, name="den")
-        for h in range(H):
-            nc.tensor.matmul(den[h * ROWS : (h + 1) * ROWS, :], ones[:], e[:, h, :], start=True, stop=True)
-        inv_den = held.tile([P, N], F32, name="inv_den")
-        nc.vector.reciprocal(inv_den[:], den[:])
+            den_col = psum.tile([N, 1], F32, name="den_col")
+            nc.tensor.matmul(den_col[:], e[:], ones[:], start=True, stop=True)
+            inv_col = work.tile([N, 1], F32, name="inv_col")
+            nc.vector.reciprocal(inv_col[:], den_col[:])
 
-        v_tiles = v_sb[:].rearrange("t (p g) -> t g p", g=G)
-        ctx_sb = [held.tile([P, N], F32, name=f"ctx_sb{g}") for g in range(G)]
-        for g in range(G):
-            ctx_ps = psum.tile([P, N], F32, name=f"ctx_ps{g}")
-            for h in range(H):
-                rows = slice(h * ROWS, (h + 1) * ROWS)
-                nc.tensor.matmul(ctx_ps[rows, :], v_tiles[:, g, rows], e[:, h, :], start=True, stop=True)
-            nc.scalar.copy(ctx_sb[g][:], ctx_ps[:])
+            ctx_ps = psum.tile([D, N], F32, name="ctx_ps")
+            nc.tensor.matmul(ctx_ps[:], v_sb[:, h * D : (h + 1) * D], e[:], start=True, stop=True)
+            ctx = work.tile([D, N], F32, name="ctx")
+            nc.vector.tensor_copy(ctx[:], ctx_ps[:])
 
-        for g in range(G):
-            nc.vector.tensor_tensor(windows[g][:].indirect(offsets[:]), ctx_sb[g][:], inv_den[:], MULT)
-            queues[g].dma_start(out_tiles[g], windows[g][:])
+            inv_ps = psum.tile([D, N], F32, name="inv_ps")
+            nc.tensor.transpose(inv_ps[:], inv_col[:].to_broadcast([N, D]), identity_f32[:])
+            inv_den = work.tile([D, N], F32, name="inv_den")
+            nc.scalar.copy(inv_den[:], inv_ps[:])
+
+            nc.vector.tensor_tensor(windows[h][:].indirect(offsets[:]), ctx[:], inv_den[:], MULT)
+            queues[h].dma_start(out[h * D : (h + 1) * D, :], windows[h][:])

@@ -21,19 +21,18 @@ def tile_multiheadattn_kernel(tc, base, q, k, v, offs, out):
         tc.tile_pool(name="work", bufs=H) as work,
         tc.psum_pool(name="psum", bufs=H) as psum,
     ):
-        queues = [nc.sync, nc.scalar]
         k_sb = [held.tile([D, N], BF16, name=f"k{h}") for h in range(H)]
         q_sb = [held.tile([D, N], BF16, name=f"q{h}") for h in range(H)]
-        windows = [held.tile([D, S], F32, name=f"window{h}") for h in range(H)]
         for h in range(H):
-            queues[h].dma_start(k_sb[h][:], k[h * D : (h + 1) * D, :])
-            queues[h].dma_start(q_sb[h][:], q[h * D : (h + 1) * D, :])
+            nc.sync.dma_start(k_sb[h][:], k[h * D : (h + 1) * D, :])
+            nc.scalar.dma_start(q_sb[h][:], q[h * D : (h + 1) * D, :])
         v_sb = held.tile([N, H * D], BF16, name="v_sb")
         nc.sync.dma_start(v_sb[:], v)
         offsets = held.tile([128, N // 16], U16, name="offsets")
         nc.sync.dma_start(offsets[:], offs)
+        windows = [held.tile([D, S], F32, name=f"window{h}") for h in range(H)]
         for h in range(H):
-            queues[h].dma_start(windows[h][:], base[h * D : (h + 1) * D, :])
+            nc.sync.dma_start(windows[h][:], base[h * D : (h + 1) * D, :])
 
         mask_f32 = held.tile([N, N], F32, name="mask_f32")
         nc.gpsimd.memset(mask_f32[:], 0.0)
@@ -50,21 +49,23 @@ def tile_multiheadattn_kernel(tc, base, q, k, v, offs, out):
         make_identity(nc, identity_f32[:], nomemset=True)
         identity = held.tile([N, N], BF16, name="identity")
         nc.vector.tensor_copy(identity[:], identity_f32[:])
-        ones = held.tile([N, 1], BF16, name="ones")
-        nc.vector.memset(ones[:], 1.0)
 
         for h in range(H):
-            scores = psum.tile([N, N], F32, name="scores")
-            nc.tensor.matmul(scores[:], identity[:], mask[:], start=True, stop=False)
-            nc.tensor.matmul(scores[:], k_sb[h][:], q_sb[h][:], start=False, stop=True)
+            scores_jt = psum.tile([N, N], F32, name="scores_jt")
+            nc.tensor.matmul(scores_jt[:], mask[:], identity[:], start=True, stop=False)
+            nc.tensor.matmul(scores_jt[:], q_sb[h][:], k_sb[h][:], start=False, stop=True)
+            scores_tj = psum.tile([N, N], F32, name="scores_tj")
+            nc.tensor.matmul(scores_tj[:], identity[:], mask[:], start=True, stop=False)
+            nc.tensor.matmul(scores_tj[:], k_sb[h][:], q_sb[h][:], start=False, stop=True)
 
-            e = work.tile([N, N], BF16, name="e")
-            nc.scalar.activation(e[:], scores[:], EXP, scale=1.0 / math.sqrt(D))
-
-            den_col = psum.tile([N, 1], F32, name="den_col")
-            nc.tensor.matmul(den_col[:], e[:], ones[:], start=True, stop=True)
+            e_jt = work.tile([N, N], BF16, name="e_jt")
+            den_col = work.tile([N, 1], F32, name="den_col")
+            nc.scalar.activation(e_jt[:], scores_jt[:], EXP, scale=1.0 / math.sqrt(D), accum_out=den_col[:])
             inv_col = work.tile([N, 1], F32, name="inv_col")
             nc.vector.reciprocal(inv_col[:], den_col[:])
+
+            e = work.tile([N, N], BF16, name="e")
+            nc.scalar.activation(e[:], scores_tj[:], EXP, scale=1.0 / math.sqrt(D))
 
             ctx_ps = psum.tile([D, N], F32, name="ctx_ps")
             nc.tensor.matmul(ctx_ps[:], v_sb[:, h * D : (h + 1) * D], e[:], start=True, stop=True)
@@ -77,4 +78,4 @@ def tile_multiheadattn_kernel(tc, base, q, k, v, offs, out):
             nc.scalar.copy(inv_den[:], inv_ps[:])
 
             nc.vector.tensor_tensor(windows[h][:].indirect(offsets[:]), ctx[:], inv_den[:], MULT)
-            queues[h].dma_start(out[h * D : (h + 1) * D, :], windows[h][:])
+            nc.sync.dma_start(out[h * D : (h + 1) * D, :], windows[h][:])

@@ -50,6 +50,12 @@ def tile_multiheadattn_kernel(tc, base, q, k, v, offs, out):
         identity = held.tile([N, N], BF16, name="identity")
         nc.vector.tensor_copy(identity[:], identity_f32[:])
 
+        def to_sbuf(h, out_sb, in_ps):
+            if h == 0:
+                nc.vector.tensor_copy(out_sb, in_ps)
+            else:
+                nc.scalar.copy(out_sb, in_ps)
+
         for h in range(H):
             scores_jt = psum.tile([N, N], F32, name="scores_jt")
             nc.tensor.matmul(scores_jt[:], mask[:], identity[:], start=True, stop=False)
@@ -70,12 +76,12 @@ def tile_multiheadattn_kernel(tc, base, q, k, v, offs, out):
             ctx_ps = psum.tile([D, N], F32, name="ctx_ps")
             nc.tensor.matmul(ctx_ps[:], v_sb[:, h * D : (h + 1) * D], e[:], start=True, stop=True)
             ctx = work.tile([D, N], F32, name="ctx")
-            nc.vector.tensor_copy(ctx[:], ctx_ps[:])
+            to_sbuf(h, ctx[:], ctx_ps[:])
 
             inv_ps = psum.tile([D, N], F32, name="inv_ps")
             nc.tensor.transpose(inv_ps[:], inv_col[:].to_broadcast([N, D]), identity_f32[:])
             inv_den = work.tile([D, N], F32, name="inv_den")
-            nc.scalar.copy(inv_den[:], inv_ps[:])
+            to_sbuf(h, inv_den[:], inv_ps[:])
 
             nc.vector.tensor_tensor(windows[h][:].indirect(offsets[:]), ctx[:], inv_den[:], MULT)
             nc.sync.dma_start(out[h * D : (h + 1) * D, :], windows[h][:])

@@ -1,12 +1,12 @@
 import math
 
 import concourse.mybir as mybir
-from concourse.masks import make_identity
 
 H, D, N, S, W = 2, 128, 128, 256, 32
 BF16, F32, U16 = mybir.dt.bfloat16, mybir.dt.float32, mybir.dt.uint16
 EXP = mybir.ActivationFunctionType.Exp
 MULT = mybir.AluOpType.mult
+SUBTRACT = mybir.AluOpType.subtract
 IS_GE = mybir.AluOpType.is_ge
 
 MASKED = -30000.0
@@ -34,21 +34,22 @@ def tile_multiheadattn_kernel(tc, base, q, k, v, offs, out):
         for h in range(H):
             nc.sync.dma_start(windows[h][:], base[h * D : (h + 1) * D, :])
 
-        mask_f32 = held.tile([N, N], F32, name="mask_f32")
-        nc.gpsimd.memset(mask_f32[:], 0.0)
+        step = held.tile([N, N + W], F32, name="step")
+        nc.gpsimd.memset(step[:], 0.0)
         nc.gpsimd.affine_select(
-            out=mask_f32[:], in_=mask_f32[:], pattern=[[1, N]], compare_op=IS_GE, fill=MASKED, base=0, channel_multiplier=-1
+            out=step[:], in_=step[:], pattern=[[1, N + W]], compare_op=IS_GE, fill=1.0, base=-W, channel_multiplier=-1
         )
-        nc.gpsimd.affine_select(
-            out=mask_f32[:], in_=mask_f32[:], pattern=[[-1, N]], compare_op=IS_GE, fill=MASKED, base=W - 1, channel_multiplier=1
-        )
-        mask = held.tile([N, N], BF16, name="mask")
-        nc.vector.tensor_copy(mask[:], mask_f32[:])
-        identity_f32 = held.tile([N, N], F32, name="identity_f32")
-        nc.vector.memset(identity_f32[:], 0.0)
-        make_identity(nc, identity_f32[:], nomemset=True)
+        near = step[:, 0:N]
+        after = step[:, W : W + N]
+        not_before = step[:, W - 1 : W - 1 + N]
         identity = held.tile([N, N], BF16, name="identity")
-        nc.vector.tensor_copy(identity[:], identity_f32[:])
+        nc.vector.tensor_tensor(identity[:], not_before, after, SUBTRACT)
+        band = held.tile([N, N], F32, name="band")
+        nc.vector.tensor_tensor(band[:], near, after, SUBTRACT)
+        mask = held.tile([N, N], BF16, name="mask")
+        nc.vector.tensor_scalar(mask[:], band[:], 1.0, -MASKED, SUBTRACT, MULT)
+        identity_f32 = held.tile([N, N], F32, name="identity_f32")
+        nc.vector.tensor_tensor(identity_f32[:], not_before, after, SUBTRACT)
 
         def to_sbuf(h, out_sb, in_ps):
             if h == 0:

@@ -8,8 +8,9 @@ EXP = mybir.ActivationFunctionType.Exp
 MULT = mybir.AluOpType.mult
 SUBTRACT = mybir.AluOpType.subtract
 IS_GE = mybir.AluOpType.is_ge
+IS_GT = mybir.AluOpType.is_gt
 
-MASKED = -30000.0
+BIG = 32768.0
 
 FLOPS = 4 * H * D * sum(min(j + 1, W) for j in range(N))
 
@@ -35,21 +36,19 @@ def tile_multiheadattn_kernel(tc, base, q, k, v, offs, out):
             nc.sync.dma_start(windows[h][:], base[h * D : (h + 1) * D, :])
 
         step = held.tile([N, N + W], F32, name="step")
-        nc.gpsimd.memset(step[:], 0.0)
+        nc.vector.memset(step[:], 0.0)
         nc.gpsimd.affine_select(
-            out=step[:], in_=step[:], pattern=[[1, N + W]], compare_op=IS_GE, fill=1.0, base=-W, channel_multiplier=-1
+            out=step[:], in_=step[:], pattern=[[1, N + W]], compare_op=IS_GE, fill=BIG, base=-W, channel_multiplier=-1
         )
         near = step[:, 0:N]
         after = step[:, W : W + N]
         not_before = step[:, W - 1 : W - 1 + N]
-        identity = held.tile([N, N], BF16, name="identity")
-        nc.vector.tensor_tensor(identity[:], not_before, after, SUBTRACT)
-        band = held.tile([N, N], F32, name="band")
-        nc.vector.tensor_tensor(band[:], near, after, SUBTRACT)
         mask = held.tile([N, N], BF16, name="mask")
-        nc.vector.tensor_scalar(mask[:], band[:], 1.0, -MASKED, SUBTRACT, MULT)
+        nc.vector.scalar_tensor_tensor(mask[:], near, BIG, after, SUBTRACT, SUBTRACT)
+        identity = held.tile([N, N], BF16, name="identity")
+        nc.vector.tensor_tensor(identity[:], not_before, after, IS_GT)
         identity_f32 = held.tile([N, N], F32, name="identity_f32")
-        nc.vector.tensor_tensor(identity_f32[:], not_before, after, SUBTRACT)
+        nc.vector.tensor_tensor(identity_f32[:], not_before, after, IS_GT)
 
         def to_sbuf(h, out_sb, in_ps):
             if h == 0:
@@ -57,32 +56,36 @@ def tile_multiheadattn_kernel(tc, base, q, k, v, offs, out):
             else:
                 nc.scalar.copy(out_sb, in_ps)
 
-        for h in range(H):
-            scores_jt = psum.tile([N, N], F32, name="scores_jt")
-            nc.tensor.matmul(scores_jt[:], mask[:], identity[:], start=True, stop=False)
-            nc.tensor.matmul(scores_jt[:], q_sb[h][:], k_sb[h][:], start=False, stop=True)
-            scores_tj = psum.tile([N, N], F32, name="scores_tj")
-            nc.tensor.matmul(scores_tj[:], identity[:], mask[:], start=True, stop=False)
-            nc.tensor.matmul(scores_tj[:], k_sb[h][:], q_sb[h][:], start=False, stop=True)
+        heads = range(H)
 
-            e_jt = work.tile([N, N], BF16, name="e_jt")
-            den_col = work.tile([N, 1], F32, name="den_col")
-            nc.scalar.activation(e_jt[:], scores_jt[:], EXP, scale=1.0 / math.sqrt(D), accum_out=den_col[:])
-            inv_col = work.tile([N, 1], F32, name="inv_col")
-            nc.vector.reciprocal(inv_col[:], den_col[:])
+        scores_jt = [psum.tile([N, N], F32, name="scores_jt") for h in heads]
+        scores_tj = [psum.tile([N, N], F32, name="scores_tj") for h in heads]
+        for h in heads:
+            nc.tensor.matmul(scores_jt[h][:], mask[:], identity[:], start=True, stop=False)
+            nc.tensor.matmul(scores_tj[h][:], identity[:], mask[:], start=True, stop=False)
+        for h in heads:
+            nc.tensor.matmul(scores_jt[h][:], q_sb[h][:], k_sb[h][:], start=False, stop=True)
+            nc.tensor.matmul(scores_tj[h][:], k_sb[h][:], q_sb[h][:], start=False, stop=True)
 
-            e = work.tile([N, N], BF16, name="e")
-            nc.scalar.activation(e[:], scores_tj[:], EXP, scale=1.0 / math.sqrt(D))
+        e_jt = [work.tile([N, N], BF16, name="e_jt") for h in heads]
+        den_col = [work.tile([N, 1], F32, name="den_col") for h in heads]
+        inv_col = [work.tile([N, 1], F32, name="inv_col") for h in heads]
+        e = [work.tile([N, N], BF16, name="e") for h in heads]
+        for h in heads:
+            nc.scalar.activation(e_jt[h][:], scores_jt[h][:], EXP, scale=1.0 / math.sqrt(D), accum_out=den_col[h][:])
+            nc.vector.reciprocal(inv_col[h][:], den_col[h][:])
+            nc.scalar.activation(e[h][:], scores_tj[h][:], EXP, scale=1.0 / math.sqrt(D))
 
-            ctx_ps = psum.tile([D, N], F32, name="ctx_ps")
-            nc.tensor.matmul(ctx_ps[:], v_sb[:, h * D : (h + 1) * D], e[:], start=True, stop=True)
-            ctx = work.tile([D, N], F32, name="ctx")
-            to_sbuf(h, ctx[:], ctx_ps[:])
+        inv_ps = [psum.tile([D, N], F32, name="inv_ps") for h in heads]
+        ctx_ps = [psum.tile([D, N], F32, name="ctx_ps") for h in heads]
+        inv_den = [work.tile([D, N], F32, name="inv_den") for h in heads]
+        ctx = [work.tile([D, N], F32, name="ctx") for h in heads]
+        for h in heads:
+            nc.tensor.transpose(inv_ps[h][:], inv_col[h][:].to_broadcast([N, D]), identity_f32[:])
+            nc.tensor.matmul(ctx_ps[h][:], v_sb[:, h * D : (h + 1) * D], e[h][:], start=True, stop=True)
+            to_sbuf(h, ctx[h][:], ctx_ps[h][:])
+            to_sbuf(h, inv_den[h][:], inv_ps[h][:])
 
-            inv_ps = psum.tile([D, N], F32, name="inv_ps")
-            nc.tensor.transpose(inv_ps[:], inv_col[:].to_broadcast([N, D]), identity_f32[:])
-            inv_den = work.tile([D, N], F32, name="inv_den")
-            to_sbuf(h, inv_den[:], inv_ps[:])
-
-            nc.vector.tensor_tensor(windows[h][:].indirect(offsets[:]), ctx[:], inv_den[:], MULT)
+        for h in heads:
+            nc.vector.tensor_tensor(windows[h][:].indirect(offsets[:]), ctx[h][:], inv_den[h][:], MULT)
             nc.sync.dma_start(out[h * D : (h + 1) * D, :], windows[h][:])

@@ -22,11 +22,12 @@ def tile_multiheadattn_kernel(tc, base, q, k, v, offs, out):
         tc.tile_pool(name="work", bufs=H) as work,
         tc.psum_pool(name="psum", bufs=H) as psum,
     ):
-        k_sb = [held.tile([D, N], BF16, name=f"k{h}") for h in range(H)]
-        q_sb = [held.tile([D, N], BF16, name=f"q{h}") for h in range(H)]
-        for h in range(H):
-            nc.sync.dma_start(k_sb[h][:], k[h * D : (h + 1) * D, :])
-            nc.scalar.dma_start(q_sb[h][:], q[h * D : (h + 1) * D, :])
+        k_all = held.tile([D, H, N], BF16, name="k_all")
+        q_all = held.tile([D, H, N], BF16, name="q_all")
+        nc.sync.dma_start(k_all[:], k.rearrange("(h d) n -> d h n", h=H))
+        nc.scalar.dma_start(q_all[:], q.rearrange("(h d) n -> d h n", h=H))
+        k_sb = [k_all[:, h, :] for h in range(H)]
+        q_sb = [q_all[:, h, :] for h in range(H)]
         v_sb = held.tile([N, H * D], BF16, name="v_sb")
         nc.sync.dma_start(v_sb[:], v)
         offsets = held.tile([128, N // 16], U16, name="offsets")
@@ -64,8 +65,8 @@ def tile_multiheadattn_kernel(tc, base, q, k, v, offs, out):
             nc.tensor.matmul(scores_jt[h][:], mask[:], identity[:], start=True, stop=False)
             nc.tensor.matmul(scores_tj[h][:], identity[:], mask[:], start=True, stop=False)
         for h in heads:
-            nc.tensor.matmul(scores_jt[h][:], q_sb[h][:], k_sb[h][:], start=False, stop=True)
-            nc.tensor.matmul(scores_tj[h][:], k_sb[h][:], q_sb[h][:], start=False, stop=True)
+            nc.tensor.matmul(scores_jt[h][:], q_sb[h], k_sb[h], start=False, stop=True)
+            nc.tensor.matmul(scores_tj[h][:], k_sb[h], q_sb[h], start=False, stop=True)
 
         e_jt = [work.tile([N, N], BF16, name="e_jt") for h in heads]
         den_col = [work.tile([N, 1], F32, name="den_col") for h in heads]

@@ -6,11 +6,14 @@ H, D, N, S, W = 2, 128, 128, 256, 32
 BF16, F32, U16 = mybir.dt.bfloat16, mybir.dt.float32, mybir.dt.uint16
 EXP = mybir.ActivationFunctionType.Exp
 MULT = mybir.AluOpType.mult
-SUBTRACT = mybir.AluOpType.subtract
-IS_GE = mybir.AluOpType.is_ge
-IS_GT = mybir.AluOpType.is_gt
+MIN = mybir.AluOpType.min
+MAX = mybir.AluOpType.max
+IS_EQUAL = mybir.AluOpType.is_equal
+NOT_EQUAL = mybir.AluOpType.not_equal
 
 BIG = 32768.0
+
+PARTS = 4
 
 FLOPS = 4 * H * D * sum(min(j + 1, W) for j in range(N))
 
@@ -22,34 +25,33 @@ def tile_multiheadattn_kernel(tc, base, q, k, v, offs, out):
         tc.tile_pool(name="work", bufs=H) as work,
         tc.psum_pool(name="psum", bufs=H) as psum,
     ):
-        k_all = held.tile([D, H, N], BF16, name="k_all")
-        q_all = held.tile([D, H, N], BF16, name="q_all")
-        nc.sync.dma_start(k_all[:], k.rearrange("(h d) n -> d h n", h=H))
-        nc.scalar.dma_start(q_all[:], q.rearrange("(h d) n -> d h n", h=H))
-        k_sb = [k_all[:, h, :] for h in range(H)]
-        q_sb = [q_all[:, h, :] for h in range(H)]
+        k_sb = [held.tile([D, N], BF16, name=f"k{h}") for h in range(H)]
+        q_sb = [held.tile([D, N], BF16, name=f"q{h}") for h in range(H)]
+        for h in range(H):
+            nc.sync.dma_start(k_sb[h][:], k[h * D : (h + 1) * D, :])
+            nc.scalar.dma_start(q_sb[h][:], q[h * D : (h + 1) * D, :])
         v_sb = held.tile([N, H * D], BF16, name="v_sb")
         nc.sync.dma_start(v_sb[:], v)
         offsets = held.tile([128, N // 16], U16, name="offsets")
         nc.sync.dma_start(offsets[:], offs)
         windows = [held.tile([D, S], F32, name=f"window{h}") for h in range(H)]
-        for h in range(H):
-            nc.sync.dma_start(windows[h][:], base[h * D : (h + 1) * D, :])
+        nc.sync.dma_start(windows[0][:], base[0:D, :])
+        part = D // PARTS
+        for d in range(0, D, part):
+            nc.sync.dma_start(windows[1][d : d + part, :], base[D + d : D + d + part, :])
 
-        step = held.tile([N, N + W], F32, name="step")
-        nc.vector.memset(step[:], 0.0)
-        nc.gpsimd.affine_select(
-            out=step[:], in_=step[:], pattern=[[1, N + W]], compare_op=IS_GE, fill=BIG, base=-W, channel_multiplier=-1
+        ramp = held.tile([N, N], BF16, name="ramp")
+        nc.gpsimd.iota(
+            ramp[:], pattern=[[1, N]], base=0, channel_multiplier=-1, allow_small_or_imprecise_dtypes=True
         )
-        near = step[:, 0:N]
-        after = step[:, W : W + N]
-        not_before = step[:, W - 1 : W - 1 + N]
-        mask = held.tile([N, N], BF16, name="mask")
-        nc.vector.scalar_tensor_tensor(mask[:], near, BIG, after, SUBTRACT, SUBTRACT)
-        identity = held.tile([N, N], BF16, name="identity")
-        nc.vector.tensor_tensor(identity[:], not_before, after, IS_GT)
+        clamped = held.tile([N, N], BF16, name="clamped")
+        nc.vector.tensor_scalar(clamped[:], ramp[:], float(W - 1), 0.0, MIN, MAX)
+        forbidden = held.tile([N, N], BF16, name="forbidden")
+        nc.vector.tensor_tensor(forbidden[:], clamped[:], ramp[:], NOT_EQUAL)
+        minus_big = held.tile([N, N], BF16, name="minus_big")
+        nc.vector.tensor_scalar(minus_big[:], ramp[:], 0.0, -BIG, IS_EQUAL, MULT)
         identity_f32 = held.tile([N, N], F32, name="identity_f32")
-        nc.vector.tensor_tensor(identity_f32[:], not_before, after, IS_GT)
+        nc.vector.tensor_scalar(identity_f32[:], ramp[:], 0.0, None, IS_EQUAL)
 
         def to_sbuf(h, out_sb, in_ps):
             if h == 0:
@@ -62,11 +64,11 @@ def tile_multiheadattn_kernel(tc, base, q, k, v, offs, out):
         scores_jt = [psum.tile([N, N], F32, name="scores_jt") for h in heads]
         scores_tj = [psum.tile([N, N], F32, name="scores_tj") for h in heads]
         for h in heads:
-            nc.tensor.matmul(scores_jt[h][:], mask[:], identity[:], start=True, stop=False)
-            nc.tensor.matmul(scores_tj[h][:], identity[:], mask[:], start=True, stop=False)
+            nc.tensor.matmul(scores_jt[h][:], forbidden[:], minus_big[:], start=True, stop=False)
+            nc.tensor.matmul(scores_tj[h][:], minus_big[:], forbidden[:], start=True, stop=False)
         for h in heads:
-            nc.tensor.matmul(scores_jt[h][:], q_sb[h], k_sb[h], start=False, stop=True)
-            nc.tensor.matmul(scores_tj[h][:], k_sb[h], q_sb[h], start=False, stop=True)
+            nc.tensor.matmul(scores_jt[h][:], q_sb[h][:], k_sb[h][:], start=False, stop=True)
+            nc.tensor.matmul(scores_tj[h][:], k_sb[h][:], q_sb[h][:], start=False, stop=True)
 
         e_jt = [work.tile([N, N], BF16, name="e_jt") for h in heads]
         den_col = [work.tile([N, 1], F32, name="den_col") for h in heads]
@@ -89,4 +91,6 @@ def tile_multiheadattn_kernel(tc, base, q, k, v, offs, out):
 
         for h in heads:
             nc.vector.tensor_tensor(windows[h][:].indirect(offsets[:]), ctx[h][:], inv_den[h][:], MULT)
-            nc.sync.dma_start(out[h * D : (h + 1) * D, :], windows[h][:])
+            store = part if h == 0 else D
+            for d in range(0, D, store):
+                nc.sync.dma_start(out[h * D + d : h * D + d + store, :], windows[h][d : d + store, :])

@@ -28,8 +28,8 @@ def tile_multiheadattn_kernel(tc, base, q, k, v, offs, out):
         k_sb = [held.tile([D, N], BF16, name=f"k{h}") for h in range(H)]
         q_sb = [held.tile([D, N], BF16, name=f"q{h}") for h in range(H)]
         for h in range(H):
+            nc.sync.dma_start(q_sb[h][:], q[h * D : (h + 1) * D, :])
             nc.sync.dma_start(k_sb[h][:], k[h * D : (h + 1) * D, :])
-            nc.scalar.dma_start(q_sb[h][:], q[h * D : (h + 1) * D, :])
         v_sb = held.tile([N, H * D], BF16, name="v_sb")
         nc.sync.dma_start(v_sb[:], v)
         offsets = held.tile([128, N // 16], U16, name="offsets")

@@ -63,12 +63,14 @@ def tile_multiheadattn_kernel(tc, base, q, k, v, offs, out):
 
         scores_jt = [psum.tile([N, N], F32, name="scores_jt") for h in heads]
         scores_tj = [psum.tile([N, N], F32, name="scores_tj") for h in heads]
-        for h in heads:
-            nc.tensor.matmul(scores_jt[h][:], forbidden[:], minus_big[:], start=True, stop=False)
-            nc.tensor.matmul(scores_tj[h][:], minus_big[:], forbidden[:], start=True, stop=False)
-        for h in heads:
-            nc.tensor.matmul(scores_jt[h][:], q_sb[h][:], k_sb[h][:], start=False, stop=True)
-            nc.tensor.matmul(scores_tj[h][:], k_sb[h][:], q_sb[h][:], start=False, stop=True)
+        nc.tensor.matmul(scores_jt[0][:], forbidden[:], minus_big[:], start=True, stop=False)
+        nc.tensor.matmul(scores_tj[0][:], minus_big[:], forbidden[:], start=True, stop=False)
+        nc.tensor.matmul(scores_jt[0][:], q_sb[0][:], k_sb[0][:], start=False, stop=True)
+        nc.tensor.matmul(scores_tj[0][:], k_sb[0][:], q_sb[0][:], start=False, stop=True)
+        nc.tensor.matmul(scores_jt[1][:], q_sb[1][:], k_sb[1][:], start=True, stop=False)
+        nc.tensor.matmul(scores_jt[1][:], forbidden[:], minus_big[:], start=False, stop=True)
+        nc.tensor.matmul(scores_tj[1][:], k_sb[1][:], q_sb[1][:], start=True, stop=False)
+        nc.tensor.matmul(scores_tj[1][:], minus_big[:], forbidden[:], start=False, stop=True)
 
         e_jt = [work.tile([N, N], BF16, name="e_jt") for h in heads]
         den_col = [work.tile([N, 1], F32, name="den_col") for h in heads]

@@ -29,7 +29,7 @@ def tile_multiheadattn_kernel(tc, base, q, k, v, offs, out):
         q_sb = [held.tile([D, N], BF16, name=f"q{h}") for h in range(H)]
         for h in range(H):
             nc.sync.dma_start(q_sb[h][:], q[h * D : (h + 1) * D, :])
-            nc.sync.dma_start(k_sb[h][:], k[h * D : (h + 1) * D, :])
+            nc.scalar.dma_start(k_sb[h][:], k[h * D : (h + 1) * D, :])
         v_sb = held.tile([N, H * D], BF16, name="v_sb")
         nc.sync.dma_start(v_sb[:], v)
         offsets = held.tile([128, N // 16], U16, name="offsets")

@@ -27,13 +27,14 @@ def tile_multiheadattn_kernel(tc, base, q, k, v, offs, out):
     ):
         k_sb = [held.tile([D, N], BF16, name=f"k{h}") for h in range(H)]
         q_sb = [held.tile([D, N], BF16, name=f"q{h}") for h in range(H)]
+        offsets = held.tile([128, N // 16], U16, name="offsets")
         for h in range(H):
             nc.sync.dma_start(q_sb[h][:], q[h * D : (h + 1) * D, :])
             nc.scalar.dma_start(k_sb[h][:], k[h * D : (h + 1) * D, :])
+            if h == 0:
+                nc.sync.dma_start(offsets[:], offs)
         v_sb = held.tile([N, H * D], BF16, name="v_sb")
         nc.sync.dma_start(v_sb[:], v)
-        offsets = held.tile([128, N // 16], U16, name="offsets")
-        nc.sync.dma_start(offsets[:], offs)
         windows = [held.tile([D, S], F32, name=f"window{h}") for h in range(H)]
         nc.sync.dma_start(windows[0][:], base[0:D, :])
         part = D // PARTS

@@ -6,10 +6,10 @@ H, D, N, S, W = 2, 128, 128, 256, 32
 BF16, F32, U16 = mybir.dt.bfloat16, mybir.dt.float32, mybir.dt.uint16
 EXP = mybir.ActivationFunctionType.Exp
 MULT = mybir.AluOpType.mult
-MIN = mybir.AluOpType.min
 MAX = mybir.AluOpType.max
 IS_EQUAL = mybir.AluOpType.is_equal
-NOT_EQUAL = mybir.AluOpType.not_equal
+IS_GT = mybir.AluOpType.is_gt
+IS_LT = mybir.AluOpType.is_lt
 
 BIG = 32768.0
 
@@ -45,12 +45,18 @@ def tile_multiheadattn_kernel(tc, base, q, k, v, offs, out):
         nc.gpsimd.iota(
             ramp[:], pattern=[[1, N]], base=0, channel_multiplier=-1, allow_small_or_imprecise_dtypes=True
         )
-        clamped = held.tile([N, N], BF16, name="clamped")
-        nc.vector.tensor_scalar(clamped[:], ramp[:], float(W - 1), 0.0, MIN, MAX)
-        forbidden = held.tile([N, N], BF16, name="forbidden")
-        nc.vector.tensor_tensor(forbidden[:], clamped[:], ramp[:], NOT_EQUAL)
         minus_big = held.tile([N, N], BF16, name="minus_big")
         nc.vector.tensor_scalar(minus_big[:], ramp[:], 0.0, -BIG, IS_EQUAL, MULT)
+        after_jt = held.tile([N, N], BF16, name="after_jt")
+        nc.vector.tensor_scalar(after_jt[:], ramp[:], 0.0, None, IS_GT)
+        after_tj = held.tile([N, N], BF16, name="after_tj")
+        nc.vector.tensor_scalar(after_tj[:], ramp[:], 0.0, None, IS_LT)
+        old_jt = held.tile([N, N], BF16, name="old_jt")
+        nc.vector.tensor_scalar(old_jt[:], ramp[:], -float(W - 1), None, IS_LT)
+        old_tj = held.tile([N, N], BF16, name="old_tj")
+        nc.vector.tensor_scalar(old_tj[:], ramp[:], float(W - 1), None, IS_GT)
+        forbidden = held.tile([N, N], BF16, name="forbidden")
+        nc.vector.tensor_tensor(forbidden[:], after_tj[:], old_tj[:], MAX)
         identity_f32 = held.tile([N, N], F32, name="identity_f32")
         nc.vector.tensor_scalar(identity_f32[:], ramp[:], 0.0, None, IS_EQUAL)
 
@@ -64,8 +70,10 @@ def tile_multiheadattn_kernel(tc, base, q, k, v, offs, out):
 
         scores_jt = [psum.tile([N, N], F32, name="scores_jt") for h in heads]
         scores_tj = [psum.tile([N, N], F32, name="scores_tj") for h in heads]
-        nc.tensor.matmul(scores_jt[0][:], forbidden[:], minus_big[:], start=True, stop=False)
-        nc.tensor.matmul(scores_tj[0][:], minus_big[:], forbidden[:], start=True, stop=False)
+        nc.tensor.matmul(scores_jt[0][:], minus_big[:], after_jt[:], start=True, stop=False)
+        nc.tensor.matmul(scores_tj[0][:], minus_big[:], after_tj[:], start=True, stop=False)
+        nc.tensor.matmul(scores_jt[0][:, 0 : N - W], minus_big[:], old_jt[:, 0 : N - W], start=False, stop=False)
+        nc.tensor.matmul(scores_tj[0][:, W:N], minus_big[:], old_tj[:, W:N], start=False, stop=False)
         nc.tensor.matmul(scores_jt[0][:], q_sb[0][:], k_sb[0][:], start=False, stop=True)
         nc.tensor.matmul(scores_tj[0][:], k_sb[0][:], q_sb[0][:], start=False, stop=True)
         nc.tensor.matmul(scores_jt[1][:], q_sb[1][:], k_sb[1][:], start=True, stop=False)

import math

import concourse.mybir as mybir

H, D, N, S, W = 2, 128, 128, 256, 32
BF16, F32, U16 = mybir.dt.bfloat16, mybir.dt.float32, mybir.dt.uint16
EXP = mybir.ActivationFunctionType.Exp
MULT = mybir.AluOpType.mult
MAX = mybir.AluOpType.max
IS_EQUAL = mybir.AluOpType.is_equal
IS_GT = mybir.AluOpType.is_gt
IS_LT = mybir.AluOpType.is_lt

BIG = 32768.0

PARTS = 4

FLOPS = 4 * H * D * sum(min(j + 1, W) for j in range(N))


def tile_multiheadattn_kernel(tc, base, q, k, v, offs, out):
    nc = tc.nc
    with (
        tc.tile_pool(name="held", bufs=1) as held,
        tc.tile_pool(name="work", bufs=H) as work,
        tc.psum_pool(name="psum", bufs=H) as psum,
    ):
        k_sb = [held.tile([D, N], BF16, name=f"k{h}") for h in range(H)]
        q_sb = [held.tile([D, N], BF16, name=f"q{h}") for h in range(H)]
        offsets = held.tile([128, N // 16], U16, name="offsets")
        for h in range(H):
            nc.sync.dma_start(q_sb[h][:], q[h * D : (h + 1) * D, :])
            nc.scalar.dma_start(k_sb[h][:], k[h * D : (h + 1) * D, :])
            if h == 0:
                nc.sync.dma_start(offsets[:], offs)
        v_sb = held.tile([N, H * D], BF16, name="v_sb")
        nc.sync.dma_start(v_sb[:], v)
        windows = [held.tile([D, S], F32, name=f"window{h}") for h in range(H)]
        nc.sync.dma_start(windows[0][:], base[0:D, :])
        part = D // PARTS
        for d in range(0, D, part):
            nc.sync.dma_start(windows[1][d : d + part, :], base[D + d : D + d + part, :])

        ramp = held.tile([N, N], BF16, name="ramp")
        nc.gpsimd.iota(
            ramp[:], pattern=[[1, N]], base=0, channel_multiplier=-1, allow_small_or_imprecise_dtypes=True
        )
        minus_big = held.tile([N, N], BF16, name="minus_big")
        nc.vector.tensor_scalar(minus_big[:], ramp[:], 0.0, -BIG, IS_EQUAL, MULT)
        after_jt = held.tile([N, N], BF16, name="after_jt")
        nc.vector.tensor_scalar(after_jt[:], ramp[:], 0.0, None, IS_GT)
        after_tj = held.tile([N, N], BF16, name="after_tj")
        nc.vector.tensor_scalar(after_tj[:], ramp[:], 0.0, None, IS_LT)
        old_jt = held.tile([N, N], BF16, name="old_jt")
        nc.vector.tensor_scalar(old_jt[:], ramp[:], -float(W - 1), None, IS_LT)
        old_tj = held.tile([N, N], BF16, name="old_tj")
        nc.vector.tensor_scalar(old_tj[:], ramp[:], float(W - 1), None, IS_GT)
        forbidden = held.tile([N, N], BF16, name="forbidden")
        nc.vector.tensor_tensor(forbidden[:], after_tj[:], old_tj[:], MAX)
        identity_f32 = held.tile([N, N], F32, name="identity_f32")
        nc.vector.tensor_scalar(identity_f32[:], ramp[:], 0.0, None, IS_EQUAL)

        def to_sbuf(h, out_sb, in_ps):
            if h == 0:
                nc.vector.tensor_copy(out_sb, in_ps)
            else:
                nc.scalar.copy(out_sb, in_ps)

        heads = range(H)

        scores_jt = [psum.tile([N, N], F32, name="scores_jt") for h in heads]
        scores_tj = [psum.tile([N, N], F32, name="scores_tj") for h in heads]
        nc.tensor.matmul(scores_jt[0][:], minus_big[:], after_jt[:], start=True, stop=False)
        nc.tensor.matmul(scores_tj[0][:], minus_big[:], after_tj[:], start=True, stop=False)
        nc.tensor.matmul(scores_jt[0][:, 0 : N - W], minus_big[:], old_jt[:, 0 : N - W], start=False, stop=False)
        nc.tensor.matmul(scores_tj[0][:, W:N], minus_big[:], old_tj[:, W:N], start=False, stop=False)
        nc.tensor.matmul(scores_jt[0][:], q_sb[0][:], k_sb[0][:], start=False, stop=True)
        nc.tensor.matmul(scores_tj[0][:], k_sb[0][:], q_sb[0][:], start=False, stop=True)
        nc.tensor.matmul(scores_jt[1][:], q_sb[1][:], k_sb[1][:], start=True, stop=False)
        nc.tensor.matmul(scores_jt[1][:], forbidden[:], minus_big[:], start=False, stop=True)
        nc.tensor.matmul(scores_tj[1][:], k_sb[1][:], q_sb[1][:], start=True, stop=False)
        nc.tensor.matmul(scores_tj[1][:], minus_big[:], forbidden[:], start=False, stop=True)

        e_jt = [work.tile([N, N], BF16, name="e_jt") for h in heads]
        den_col = [work.tile([N, 1], F32, name="den_col") for h in heads]
        inv_col = [work.tile([N, 1], F32, name="inv_col") for h in heads]
        e = [work.tile([N, N], BF16, name="e") for h in heads]
        for h in heads:
            nc.scalar.activation(e_jt[h][:], scores_jt[h][:], EXP, scale=1.0 / math.sqrt(D), accum_out=den_col[h][:])
            nc.vector.reciprocal(inv_col[h][:], den_col[h][:])
            nc.scalar.activation(e[h][:], scores_tj[h][:], EXP, scale=1.0 / math.sqrt(D))

        inv_ps = [psum.tile([D, N], F32, name="inv_ps") for h in heads]
        ctx_ps = [psum.tile([D, N], F32, name="ctx_ps") for h in heads]
        inv_den = [work.tile([D, N], F32, name="inv_den") for h in heads]
        ctx = [work.tile([D, N], F32, name="ctx") for h in heads]
        for h in heads:
            nc.tensor.transpose(inv_ps[h][:], inv_col[h][:].to_broadcast([N, D]), identity_f32[:])
            nc.tensor.matmul(ctx_ps[h][:], v_sb[:, h * D : (h + 1) * D], e[h][:], start=True, stop=True)
            to_sbuf(h, ctx[h][:], ctx_ps[h][:])
            to_sbuf(h, inv_den[h][:], inv_ps[h][:])

        for h in heads:
            nc.vector.tensor_tensor(windows[h][:].indirect(offsets[:]), ctx[h][:], inv_den[h][:], MULT)
            store = part if h == 0 else D
            for d in range(0, D, store):
                nc.sync.dma_start(out[h * D + d : h * D + d + store, :], windows[h][d : d + store, :])
